import numpy as np
import ml_dtypes


def mxq(x, axis, fmt="e4m3"):
    dtype, down = {"e4m3": (ml_dtypes.float8_e4m3fn, 7), "e5m2": (ml_dtypes.float8_e5m2, 14)}[fmt]
    v = np.moveaxis(np.asarray(x, np.float32).astype(ml_dtypes.bfloat16).astype(np.float64), axis, -1)
    blocks = v.reshape(v.shape[:-1] + (-1, 32))
    amax = np.abs(blocks).max(-1, keepdims=True)
    byte = np.maximum(np.where(amax > 0, np.frexp(amax)[1] - 1 + 127, 0) - down, 1)
    scale = np.exp2(byte - 127.0)
    codes = (blocks / scale).astype(np.float32).astype(dtype).astype(np.float64)
    return np.moveaxis((codes * scale).reshape(v.shape), -1, axis)


WIDE = False


def mx_kscale(k):
    if not WIDE:
        return np.ones(k)
    levels = np.array([10, -10, 5, -5, 0])
    a = np.random.permutation(np.resize(levels, k // 512 * 4)).reshape(k // 512, 4)
    idx = np.arange(k)
    return np.exp2(a[idx // 512, idx % 128 // 32])


BF16 = ml_dtypes.bfloat16


def bf(x):
    return np.asarray(x, np.float32).astype(BF16)


def f64(x):
    return np.asarray(x).astype(np.float64)


E2M1 = np.array([0.0, 0.5, 1.0, 1.5, 2.0, 3.0, 4.0, 6.0, -0.0, -0.5, -1.0, -1.5, -2.0, -3.0, -4.0, -6.0])


def pack_weight(w, fmt):
    k, n = w.shape
    w = f64(bf(w)).reshape(k // 32, 32, n)
    amax = np.abs(w).max(1)
    if fmt == "e4m3":
        byte = np.frexp(amax)[1] - 1 + 127 - 7
    else:
        mant, ex = np.frexp(amax / 6.0)
        byte = np.where(mant > 0.5, ex, ex - 1) + 127
    byte = np.clip(np.where(amax > 0, byte, 1), 1, 254)
    scaled = (w * np.exp2(127.0 - byte)[:, None, :]).reshape(k, n).astype(np.float32)
    by_word = np.ascontiguousarray(scaled.reshape(k // 512, 128, 4, n).transpose(0, 1, 3, 2))
    if fmt == "e4m3":
        words = by_word.astype(ml_dtypes.float8_e4m3fn).view(np.uint8)
    else:
        c = by_word.astype(ml_dtypes.float4_e2m1fn).view(np.uint8) & 0xF
        words = c[..., 0::2] | (c[..., 1::2] << 4)
    return np.ascontiguousarray(words), np.ascontiguousarray(byte.astype(np.uint8).reshape(k // 512, 16, n))


def unpack_weight(words, scales, fmt):
    g, p, n, _ = words.shape
    if fmt == "e4m3":
        vals = np.ascontiguousarray(words).view(ml_dtypes.float8_e4m3fn).astype(np.float64)
    else:
        nib = np.empty((g, p, n, 4), np.uint8)
        nib[..., 0::2] = words & 0xF
        nib[..., 1::2] = words >> 4
        vals = E2M1[nib]
    vals = vals * np.repeat(np.exp2(scales.astype(np.float64) - 127.0), 8, axis=1)[..., None]
    return vals.transpose(0, 1, 3, 2).reshape(g * 512, n)


B, S, D, H, KD, VD = 8, 32, 8192, 8, 128, 128
E = H * VD
EPS = 1e-5
FMT = "e4m3"


def silu(v):
    return v / (1.0 + np.exp(-v))


def setup_inputs():
    s = mx_kscale(D)
    amp = 10.0 ** np.random.uniform(-2.5, 0.5, (B, S, H, 1))
    ret = amp * (np.random.standard_normal((B, S, H, VD)) + 0.3 * np.random.standard_normal((B, S, H, 1)))
    x = bf(np.random.standard_normal((B, S, D)) * s)
    ret_cat = bf(ret.reshape(B, S, E))
    Wg_words, Wg_scales = pack_weight(np.random.standard_normal((D, E)) / np.sqrt(D) / s[:, None], FMT)
    bg = bf(np.random.standard_normal(E) * 0.2)
    Wo_words, Wo_scales = pack_weight(np.random.standard_normal((E, D)) / np.sqrt(E), FMT)
    bo = bf(np.random.standard_normal(D) * 0.2)
    return {"x": x,
            "ret_cat": ret_cat,
            "Wg_words": Wg_words,
            "Wg_scales": Wg_scales,
            "bg": bg,
            "Wo_words": Wo_words,
            "Wo_scales": Wo_scales,
            "bo": bo}


def reference(x, ret_cat, Wg_words, Wg_scales, bg, Wo_words, Wo_scales, bo):
    gate = silu((mxq(f64(x), 2, "e4m3") @ unpack_weight(Wg_words, Wg_scales, FMT)) + f64(bg))
    g = f64(ret_cat).reshape(B * S, H, VD)
    mu = g.mean(-1, keepdims=True)
    var = g.var(-1, keepdims=True)
    cat = ((g - mu) / np.sqrt(var + EPS)).reshape(B, S, E)
    h = gate * cat
    return (mxq(h, 2, "e4m3") @ unpack_weight(Wo_words, Wo_scales, FMT)) + f64(bo)

@@ -1,0 +1,337 @@
+from contextlib import ExitStack
+
+import concourse.mybir as mybir
+from concourse.masks import make_identity
+
+F32 = mybir.dt.float32
+BF16 = mybir.dt.bfloat16
+I32 = mybir.dt.int32
+U32 = mybir.dt.uint32
+U8 = mybir.dt.uint8
+FP8X4 = mybir.dt.float8_e4m3fn_x4
+ADD = mybir.AluOpType.add
+MULT = mybir.AluOpType.mult
+ACT = mybir.ActivationFunctionType
+
+P = 128
+PACK = 4
+K_PASS = P * PACK
+N_PASS = 512
+
+TOKENS = 256
+TOKEN_TILES = TOKENS // P
+D = 8192
+E = 1024
+GROUP = 128
+EPS = 1e-5
+
+X_PASSES = D // K_PASS
+H_PASSES = E // K_PASS
+E_BANKS = E // N_PASS
+PLANES = 4
+QUADS = 4
+
+CHUNK_COLS = 2048
+X_CHUNKS = D // CHUNK_COLS
+PASSES_PER_X_CHUNK = CHUNK_COLS // K_PASS
+WG_CHUNK_PASSES = 2
+WG_CHUNKS = X_PASSES // WG_CHUNK_PASSES
+WO_CHUNK_COLS = 1024
+WO_CHUNKS = D // WO_CHUNK_COLS
+SCALE_LOADS_PER_BIG_LOAD = 2
+
+FLOPS = 2 * TOKENS * D * E * 2
+
+
+def tile_gatedmultiscaleretentionlayer_pa_k_kernel(
+    tc, x, ret_cat, Wg_words, Wg_scales, bg, Wo_words, Wo_scales, bo, out
+):
+    nc = tc.nc
+
+    x_view = x.rearrange("b s d -> (b s) d").rearrange("(i p) d -> p i d", p=P)
+    ret_view = ret_cat.rearrange("b s e -> (b s) e").rearrange("(i p) e -> p i e", p=P)
+    out_view = out.rearrange("b s d -> (b s) d").rearrange("(i p) d -> p i d", p=P)
+    wg_view = Wg_words.rearrange("g p n t -> p g (n t)")
+    wo_view = Wo_words.rearrange("g p n t -> p g (n t)")
+
+    with ExitStack() as stack:
+        stack.enter_context(tc.manual_schedule())
+        keep = stack.enter_context(tc.tile_pool(name="keep", bufs=1))
+        chunks = stack.enter_context(tc.tile_pool(name="chunks", bufs=16))
+        stage = stack.enter_context(tc.tile_pool(name="stage", bufs=3))
+        acc_pool = stack.enter_context(tc.psum_pool(name="acc", bufs=4))
+        work_pool = stack.enter_context(tc.psum_pool(name="work", bufs=4))
+
+        bias_rows = keep.tile([P, N_PASS], BF16)
+        nc.vector.memset(bias_rows[:], 0.0)
+        wg_planes = keep.tile([P, X_PASSES // PLANES, E], U8, align_bytes=64)
+        wo_planes = keep.tile([P, H_PASSES, D // PLANES], U8, align_bytes=64)
+        nc.vector.memset(wg_planes[:].rearrange("p a n -> p (a n)").bitcast(I32), 0)
+        nc.vector.memset(wo_planes[:].rearrange("p a n -> p (a n)").bitcast(I32), 0)
+
+        ident_bf = keep.tile([P, P], BF16)
+        make_identity(nc, ident_bf[:])
+        ident_f32 = keep.tile([P, P], F32)
+        make_identity(nc, ident_f32[:])
+
+        x_codes = keep.tile([P, X_PASSES, TOKENS], U32, align_bytes=64)
+        x_planes = keep.tile([P, X_PASSES, TOKENS], U8, align_bytes=64)
+        h_codes = keep.tile([P, H_PASSES, TOKENS], U32, align_bytes=64)
+        h_planes = keep.tile([P, H_PASSES, TOKENS], U8, align_bytes=64)
+        bo_all = keep.tile([P, D], BF16)
+        bg_all = keep.tile([P, E], BF16)
+
+        bo_rows = D // N_PASS
+        bg_rows = E // N_PASS
+        nc.sync.dma_start(out=bias_rows[0:bo_rows, :], in_=bo.rearrange("(r c) -> r c", c=N_PASS))
+        nc.sync.dma_start(
+            out=bias_rows[bo_rows : bo_rows + bg_rows, :], in_=bg.rearrange("(r c) -> r c", c=N_PASS)
+        )
+
+        scale_loads = []
+        for a in range(X_PASSES // PLANES):
+            for q in range(QUADS):
+                scale_loads.append(
+                    (
+                        wg_planes[32 * q : 32 * q + 16, a, :].bitcast(I32),
+                        Wg_scales[PLANES * a : PLANES * (a + 1), 4 * q : 4 * q + 4, :].bitcast(I32),
+                    )
+                )
+        for g in range(H_PASSES):
+            for q in range(QUADS):
+                scale_loads.append(
+                    (
+                        wo_planes[32 * q : 32 * q + 16, g, :].bitcast(I32),
+                        Wo_scales[g, 4 * q : 4 * q + 4, :]
+                        .rearrange("r (j n) -> j r n", j=PLANES)
+                        .bitcast(I32),
+                    )
+                )
+
+        def big_load(index, dst, src):
+            nc.sync.dma_start(out=dst, in_=src)
+            first = SCALE_LOADS_PER_BIG_LOAD * index
+            for plane_dst, plane_src in scale_loads[first : first + SCALE_LOADS_PER_BIG_LOAD]:
+                nc.sync.dma_start(out=plane_dst, in_=plane_src)
+
+        x_chunks = []
+        for c in range(X_CHUNKS):
+            x_chunk = chunks.tile([P, TOKEN_TILES, CHUNK_COLS], BF16, tag="chunk", name="x_chunk", align_bytes=64)
+            big_load(c, x_chunk[:], x_view[:, :, CHUNK_COLS * c : CHUNK_COLS * (c + 1)])
+            x_chunks.append(x_chunk)
+
+        ret_sb = keep.tile([P, TOKEN_TILES, E], BF16)
+        big_load(X_CHUNKS, ret_sb[:], ret_view)
+
+        wg_chunks = []
+        for c in range(WG_CHUNKS):
+            wg_chunk = chunks.tile(
+                [P, WG_CHUNK_PASSES, E], U32, tag="chunk", name="wg_chunk", align_bytes=64
+            )
+            big_load(
+                X_CHUNKS + 1 + c,
+                wg_chunk[:].bitcast(I32),
+                wg_view[:, WG_CHUNK_PASSES * c : WG_CHUNK_PASSES * (c + 1), :].bitcast(I32),
+            )
+            wg_chunks.append(wg_chunk)
+        assert SCALE_LOADS_PER_BIG_LOAD * (X_CHUNKS + 1 + WG_CHUNKS) >= len(scale_loads)
+
+        def spread_bias(first_row, dst):
+            picked = work_pool.tile([P, 2 * N_PASS], BF16, tag="work", name="picked")
+            for i in range(2):
+                nc.tensor.matmul(
+                    out=picked[:, N_PASS * i : N_PASS * (i + 1)],
+                    lhsT=ident_bf[:, first_row + i : first_row + i + 1].to_broadcast([P, P]),
+                    rhs=bias_rows[:],
+                    start=True,
+                    stop=True,
+                )
+            nc.scalar.copy(out=dst, in_=picked[:])
+
+        spread_bias(bo_rows, bg_all[:])
+        for r in range(0, bo_rows, 2):
+            spread_bias(r, bo_all[:, N_PASS * r : N_PASS * (r + 2)])
+
+        def transpose_x_pass(g, grouped_words, copy):
+            c, g_in_chunk = divmod(g, PASSES_PER_X_CHUNK)
+            halves = work_pool.tile([P, 2, TOKENS], F32, tag="work", name="halves")
+            first_word = (K_PASS // 2) * g_in_chunk
+            for i in range(TOKEN_TILES):
+                words = x_chunks[c][:, i, :].bitcast(F32)
+                for u in range(2):
+                    nc.tensor.transpose(
+                        halves[:, u, P * i : P * (i + 1)],
+                        words[:, first_word + u : first_word + K_PASS // 2 : 2],
+                        ident_f32[:],
+                    )
+            copy(
+                out=grouped_words.rearrange("p (w u) -> p w u", u=2),
+                in_=halves[:].rearrange("p u w -> p w u"),
+            )
+
+        def quantise_x_pair(pair, grouped):
+            passes = slice(2 * pair, 2 * pair + 2)
+            nc.vector.quantize_mx(
+                out=x_codes[:, passes, :].rearrange("p g w -> p (g w)").bitcast(FP8X4),
+                scales=x_planes[:, passes, :].rearrange("p g w -> p (g w)"),
+                in_=grouped[:].rearrange("p g v -> p (g v)"),
+            )
+
+        grouped_pairs = []
+        for pair in range(X_PASSES // 2):
+            grouped = stage.tile([P, 2, TOKENS * PACK], BF16, name="grouped", align_bytes=64)
+            grouped_pairs.append(grouped)
+            transpose_x_pass(2 * pair, grouped[:, 0, :].bitcast(F32), nc.scalar.copy)
+            transpose_x_pass(2 * pair + 1, grouped[:, 1, :].bitcast(F32), nc.vector.tensor_copy)
+            if pair > 0:
+                quantise_x_pair(pair - 1, grouped_pairs[pair - 1])
+        quantise_x_pair(X_PASSES // 2 - 1, grouped_pairs[-1])
+
+        wo_chunks = []
+        for c in range(WO_CHUNKS):
+            wo_chunk = chunks.tile(
+                [P, H_PASSES, WO_CHUNK_COLS], U32, tag="chunk", name="wo_chunk", align_bytes=64
+            )
+            nc.sync.dma_start(
+                out=wo_chunk[:].bitcast(I32),
+                in_=wo_view[
+                    :, :, PACK * WO_CHUNK_COLS * c : PACK * WO_CHUNK_COLS * (c + 1)
+                ].bitcast(I32),
+            )
+            wo_chunks.append(wo_chunk)
+
+        n_groups = TOKEN_TILES * E // GROUP
+        by_group = ret_sb[:].rearrange("p i (h c) -> p (i h) c", c=GROUP)
+        sums = keep.tile([P, n_groups], F32)
+        nc.vector.tensor_reduce(out=sums[:], in_=by_group, axis=mybir.AxisListType.X, op=ADD)
+        neg_mean = keep.tile([P, n_groups], F32)
+        nc.vector.tensor_scalar(
+            out=neg_mean[:], in0=sums[:], scalar1=-1.0 / GROUP, scalar2=None, op0=MULT
+        )
+        cat = keep.tile([P, n_groups, GROUP], F32)
+        nc.vector.tensor_tensor(
+            out=cat[:],
+            in0=by_group,
+            in1=neg_mean[:].unsqueeze(2).to_broadcast([P, n_groups, GROUP]),
+            op=ADD,
+        )
+        squares = keep.tile([P, n_groups, GROUP], F32)
+        nc.scalar.activation(out=squares[:], in_=cat[:], func=ACT.Square)
+        square_sums = keep.tile([P, n_groups], F32)
+        nc.vector.tensor_reduce(
+            out=square_sums[:], in_=squares[:], axis=mybir.AxisListType.X, op=ADD
+        )
+        var_eps = keep.tile([P, n_groups], F32)
+        nc.vector.tensor_scalar(
+            out=var_eps[:], in0=square_sums[:], scalar1=1.0 / GROUP, scalar2=EPS, op0=MULT, op1=ADD
+        )
+        std = keep.tile([P, n_groups], F32)
+        nc.scalar.activation(out=std[:], in_=var_eps[:], func=ACT.Sqrt)
+        table_warmer = keep.tile([P, 1], F32)
+        nc.scalar.activation(out=table_warmer[:], in_=std[:, 0:1], func=ACT.Silu)
+        inv_std = keep.tile([P, n_groups], F32)
+        nc.vector.reciprocal(out=inv_std[:], in_=std[:])
+        nc.vector.tensor_tensor(
+            out=cat[:],
+            in0=cat[:],
+            in1=inv_std[:].unsqueeze(2).to_broadcast([P, n_groups, GROUP]),
+            op=MULT,
+        )
+        cat_flat = cat[:].rearrange("p (i h) c -> p i (h c)", i=TOKEN_TILES)
+
+        gate_banks = [(i, b) for i in range(TOKEN_TILES) for b in range(E_BANKS)]
+        gate_acc = [
+            acc_pool.tile([P, N_PASS], F32, tag="acc", name="gate_acc") for bank in gate_banks
+        ]
+        for g in range(X_PASSES):
+            wg_chunk = wg_chunks[g // WG_CHUNK_PASSES]
+            block, plane = divmod(g, PLANES)
+            for acc, (i, b) in zip(gate_acc, gate_banks):
+                tokens = slice(P * i, P * (i + 1))
+                cols = slice(N_PASS * b, N_PASS * (b + 1))
+                nc.tensor.matmul_mx(
+                    out=acc[:],
+                    lhsT=x_codes[:, g, tokens].bitcast(FP8X4),
+                    lhsT_scale=x_planes[:, g, tokens],
+                    rhs=wg_chunk[:, g % WG_CHUNK_PASSES, cols].bitcast(FP8X4),
+                    rhs_scale=wg_planes[4 * plane : P, block, cols],
+                    start=(g == 0),
+                    stop=(g == X_PASSES - 1),
+                )
+
+        gates = {}
+        h_grouped = {}
+
+        def add_bias_and_silu(n):
+            i, b = gate_banks[n]
+            gate = stage.tile([P, N_PASS], F32, name="gate")
+            nc.vector.tensor_tensor(
+                out=gate[:], in0=gate_acc[n][:], in1=bg_all[:, N_PASS * b : N_PASS * (b + 1)], op=ADD
+            )
+            nc.scalar.activation(out=gate[:], in_=gate[:], func=ACT.Silu)
+            gates[n] = gate
+
+        def multiply_and_transpose(n):
+            i, b = gate_banks[n]
+            h_runs = stage.tile([P, PACK, P], BF16, name="h_runs")
+            nc.vector.tensor_tensor(
+                out=h_runs[:],
+                in0=gates[n][:].rearrange("p (c t) -> p t c", t=PACK),
+                in1=cat_flat[:, i, N_PASS * b : N_PASS * (b + 1)].rearrange("p (c t) -> p t c", t=PACK),
+                op=MULT,
+            )
+            flipped = work_pool.tile([P, PACK, P], BF16, tag="work", name="flipped")
+            for t in range(PACK):
+                nc.tensor.transpose(flipped[:, t, :], h_runs[:, t, :], ident_bf[:])
+            grouped_h = stage.tile([P, P, PACK], BF16, name="grouped_h", align_bytes=64)
+            nc.scalar.copy(out=grouped_h[:], in_=flipped[:].rearrange("p t w -> p w t"))
+            h_grouped[n] = grouped_h
+
+        def quantise_h(n):
+            i, b = gate_banks[n]
+            tokens = slice(P * i, P * (i + 1))
+            nc.vector.quantize_mx(
+                out=h_codes[:, b, tokens].bitcast(FP8X4),
+                scales=h_planes[:, b, tokens],
+                in_=h_grouped[n][:].rearrange("p w t -> p (w t)"),
+            )
+
+        n_banks = len(gate_banks)
+        for n in range(n_banks + 2):
+            if n < n_banks:
+                add_bias_and_silu(n)
+            if 1 <= n <= n_banks:
+                multiply_and_transpose(n - 1)
+            if n >= 2:
+                quantise_h(n - 2)
+
+        for c in range(WO_CHUNKS):
+            out_chunk = chunks.tile(
+                [P, TOKEN_TILES, WO_CHUNK_COLS], F32, tag="chunk", name="out_chunk", align_bytes=64
+            )
+            for i in range(TOKEN_TILES):
+                tokens = slice(P * i, P * (i + 1))
+                for b in range(WO_CHUNK_COLS // N_PASS):
+                    cols = slice(N_PASS * b, N_PASS * (b + 1))
+                    first_col = WO_CHUNK_COLS * c + N_PASS * b
+                    plane, plane_col = divmod(first_col, D // PLANES)
+                    product = acc_pool.tile([P, N_PASS], F32, tag="acc", name="product")
+                    for g in range(H_PASSES):
+                        nc.tensor.matmul_mx(
+                            out=product[:],
+                            lhsT=h_codes[:, g, tokens].bitcast(FP8X4),
+                            lhsT_scale=h_planes[:, g, tokens],
+                            rhs=wo_chunks[c][:, g, cols].bitcast(FP8X4),
+                            rhs_scale=wo_planes[4 * plane : P, g, plane_col : plane_col + N_PASS],
+                            start=(g == 0),
+                            stop=(g == H_PASSES - 1),
+                        )
+                    nc.vector.tensor_tensor(
+                        out=out_chunk[:, i, cols],
+                        in0=product[:],
+                        in1=bo_all[:, first_col : first_col + N_PASS],
+                        op=ADD,
+                    )
+            nc.sync.dma_start(
+                out=out_view[:, :, WO_CHUNK_COLS * c : WO_CHUNK_COLS * (c + 1)], in_=out_chunk[:]
+            )

@@ -38,7 +38,6 @@ WG_CHUNK_PASSES = 2
 WG_CHUNKS = X_PASSES // WG_CHUNK_PASSES
 WO_CHUNK_COLS = 1024
 WO_CHUNKS = D // WO_CHUNK_COLS
-SCALE_LOADS_PER_BIG_LOAD = 2
 
 FLOPS = 2 * TOKENS * D * E * 2
 
@@ -88,53 +87,42 @@ def tile_gatedmultiscaleretentionlayer_pa_k_kernel(
             out=bias_rows[bo_rows : bo_rows + bg_rows, :], in_=bg.rearrange("(r c) -> r c", c=N_PASS)
         )
 
-        scale_loads = []
         for a in range(X_PASSES // PLANES):
             for q in range(QUADS):
-                scale_loads.append(
-                    (
-                        wg_planes[32 * q : 32 * q + 16, a, :].bitcast(I32),
-                        Wg_scales[PLANES * a : PLANES * (a + 1), 4 * q : 4 * q + 4, :].bitcast(I32),
-                    )
+                nc.gpsimd.dma_start(
+                    out=wg_planes[32 * q : 32 * q + 16, a, :].bitcast(F32),
+                    in_=Wg_scales[PLANES * a : PLANES * (a + 1), 4 * q : 4 * q + 4, :].bitcast(F32),
                 )
         for g in range(H_PASSES):
             for q in range(QUADS):
-                scale_loads.append(
-                    (
-                        wo_planes[32 * q : 32 * q + 16, g, :].bitcast(I32),
-                        Wo_scales[g, 4 * q : 4 * q + 4, :]
-                        .rearrange("r (j n) -> j r n", j=PLANES)
-                        .bitcast(I32),
-                    )
+                nc.gpsimd.dma_start(
+                    out=wo_planes[32 * q : 32 * q + 16, g, :].bitcast(F32),
+                    in_=Wo_scales[g, 4 * q : 4 * q + 4, :]
+                    .rearrange("r (j n) -> j r n", j=PLANES)
+                    .bitcast(F32),
                 )
-
-        def big_load(index, dst, src):
-            nc.sync.dma_start(out=dst, in_=src)
-            first = SCALE_LOADS_PER_BIG_LOAD * index
-            for plane_dst, plane_src in scale_loads[first : first + SCALE_LOADS_PER_BIG_LOAD]:
-                nc.sync.dma_start(out=plane_dst, in_=plane_src)
 
         x_chunks = []
         for c in range(X_CHUNKS):
             x_chunk = chunks.tile([P, TOKEN_TILES, CHUNK_COLS], BF16, tag="chunk", name="x_chunk", align_bytes=64)
-            big_load(c, x_chunk[:], x_view[:, :, CHUNK_COLS * c : CHUNK_COLS * (c + 1)])
+            nc.sync.dma_start(
+                out=x_chunk[:], in_=x_view[:, :, CHUNK_COLS * c : CHUNK_COLS * (c + 1)]
+            )
             x_chunks.append(x_chunk)
 
         ret_sb = keep.tile([P, TOKEN_TILES, E], BF16)
-        big_load(X_CHUNKS, ret_sb[:], ret_view)
+        nc.sync.dma_start(out=ret_sb[:], in_=ret_view)
 
         wg_chunks = []
         for c in range(WG_CHUNKS):
             wg_chunk = chunks.tile(
                 [P, WG_CHUNK_PASSES, E], U32, tag="chunk", name="wg_chunk", align_bytes=64
             )
-            big_load(
-                X_CHUNKS + 1 + c,
-                wg_chunk[:].bitcast(I32),
-                wg_view[:, WG_CHUNK_PASSES * c : WG_CHUNK_PASSES * (c + 1), :].bitcast(I32),
+            nc.sync.dma_start(
+                out=wg_chunk[:].bitcast(I32),
+                in_=wg_view[:, WG_CHUNK_PASSES * c : WG_CHUNK_PASSES * (c + 1), :].bitcast(I32),
             )
             wg_chunks.append(wg_chunk)
-        assert SCALE_LOADS_PER_BIG_LOAD * (X_CHUNKS + 1 + WG_CHUNKS) >= len(scale_loads)
 
         def spread_bias(first_row, dst):
             picked = work_pool.tile([P, 2 * N_PASS], BF16, tag="work", name="picked")

@@ -82,11 +82,6 @@ def tile_gatedmultiscaleretentionlayer_pa_k_kernel(
 
         bo_rows = D // N_PASS
         bg_rows = E // N_PASS
-        nc.sync.dma_start(out=bias_rows[0:bo_rows, :], in_=bo.rearrange("(r c) -> r c", c=N_PASS))
-        nc.sync.dma_start(
-            out=bias_rows[bo_rows : bo_rows + bg_rows, :], in_=bg.rearrange("(r c) -> r c", c=N_PASS)
-        )
-
         for a in range(X_PASSES // PLANES):
             for q in range(QUADS):
                 nc.gpsimd.dma_start(
@@ -109,6 +104,11 @@ def tile_gatedmultiscaleretentionlayer_pa_k_kernel(
                 out=x_chunk[:], in_=x_view[:, :, CHUNK_COLS * c : CHUNK_COLS * (c + 1)]
             )
             x_chunks.append(x_chunk)
+            if c == 0:
+                nc.sync.dma_start(out=bias_rows[0:bo_rows, :], in_=bo.rearrange("(r c) -> r c", c=N_PASS))
+                nc.sync.dma_start(
+                    out=bias_rows[bo_rows : bo_rows + bg_rows, :], in_=bg.rearrange("(r c) -> r c", c=N_PASS)
+                )
 
         ret_sb = keep.tile([P, TOKEN_TILES, E], BF16)
         nc.sync.dma_start(out=ret_sb[:], in_=ret_view)
@@ -136,8 +136,7 @@ def tile_gatedmultiscaleretentionlayer_pa_k_kernel(
                 )
             nc.scalar.copy(out=dst, in_=picked[:])
 
-        spread_bias(bo_rows, bg_all[:])
-        for r in range(0, bo_rows, 2):
+        def spread_bo(r):
             spread_bias(r, bo_all[:, N_PASS * r : N_PASS * (r + 2)])
 
         def transpose_x_pass(g, grouped_words, copy):
@@ -173,6 +172,10 @@ def tile_gatedmultiscaleretentionlayer_pa_k_kernel(
             transpose_x_pass(2 * pair + 1, grouped[:, 1, :].bitcast(F32), nc.vector.tensor_copy)
             if pair > 0:
                 quantise_x_pair(pair - 1, grouped_pairs[pair - 1])
+            if pair == 1:
+                spread_bias(bo_rows, bg_all[:])
+            if pair >= 2:
+                spread_bo(2 * (pair - 2))
         quantise_x_pair(X_PASSES // 2 - 1, grouped_pairs[-1])
 
         wo_chunks = []
@@ -231,10 +234,11 @@ def tile_gatedmultiscaleretentionlayer_pa_k_kernel(
         gate_acc = [
             acc_pool.tile([P, N_PASS], F32, tag="acc", name="gate_acc") for bank in gate_banks
         ]
-        for g in range(X_PASSES):
-            wg_chunk = wg_chunks[g // WG_CHUNK_PASSES]
-            block, plane = divmod(g, PLANES)
-            for acc, (i, b) in zip(gate_acc, gate_banks):
+        for c in range(WG_CHUNKS):
+          wg_chunk = wg_chunks[c]
+          for acc, (i, b) in zip(gate_acc, gate_banks):
+            for g in range(WG_CHUNK_PASSES * c, WG_CHUNK_PASSES * (c + 1)):
+                block, plane = divmod(g, PLANES)
                 tokens = slice(P * i, P * (i + 1))
                 cols = slice(N_PASS * b, N_PASS * (b + 1))
                 nc.tensor.matmul_mx(
@@ -246,6 +250,8 @@ def tile_gatedmultiscaleretentionlayer_pa_k_kernel(
                     start=(g == 0),
                     stop=(g == X_PASSES - 1),
                 )
+          if c < 2:
+            spread_bo(12 + 2 * c)
 
         gates = {}
         h_grouped = {}

@@ -31,13 +31,13 @@ E_BANKS = E // N_PASS
 PLANES = 4
 QUADS = 4
 
-CHUNK_COLS = 2048
-X_CHUNKS = D // CHUNK_COLS
-PASSES_PER_X_CHUNK = CHUNK_COLS // K_PASS
-WG_CHUNK_PASSES = 2
-WG_CHUNKS = X_PASSES // WG_CHUNK_PASSES
-WO_CHUNK_COLS = 1024
-WO_CHUNKS = D // WO_CHUNK_COLS
+X_LOAD_COLS = 4096
+WG_TILE_PASSES = 4
+WG_LOAD_PASSES = 2
+WG_LOADS = X_PASSES // WG_LOAD_PASSES
+WO_COLS = 4096
+OUT_COLS = 4096
+STORE_COLS = 2048
 
 FLOPS = 2 * TOKENS * D * E * 2
 
@@ -56,7 +56,7 @@ def tile_gatedmultiscaleretentionlayer_pa_k_kernel(
     with ExitStack() as stack:
         stack.enter_context(tc.manual_schedule())
         keep = stack.enter_context(tc.tile_pool(name="keep", bufs=1))
-        chunks = stack.enter_context(tc.tile_pool(name="chunks", bufs=16))
+        chunks = stack.enter_context(tc.tile_pool(name="chunks", bufs=8))
         stage = stack.enter_context(tc.tile_pool(name="stage", bufs=3))
         acc_pool = stack.enter_context(tc.psum_pool(name="acc", bufs=4))
         work_pool = stack.enter_context(tc.psum_pool(name="work", bufs=4))
@@ -73,8 +73,8 @@ def tile_gatedmultiscaleretentionlayer_pa_k_kernel(
         ident_f32 = keep.tile([P, P], F32)
         make_identity(nc, ident_f32[:])
 
-        x_codes = keep.tile([P, X_PASSES, TOKENS], U32, align_bytes=64)
-        x_planes = keep.tile([P, X_PASSES, TOKENS], U8, align_bytes=64)
+        x_codes = keep.tile([P, TOKEN_TILES, X_PASSES, P], U32, align_bytes=64)
+        x_planes = keep.tile([P, TOKEN_TILES, X_PASSES, P], U8, align_bytes=64)
         h_codes = keep.tile([P, H_PASSES, TOKENS], U32, align_bytes=64)
         h_planes = keep.tile([P, H_PASSES, TOKENS], U8, align_bytes=64)
         bo_all = keep.tile([P, D], BF16)
@@ -97,32 +97,40 @@ def tile_gatedmultiscaleretentionlayer_pa_k_kernel(
                     .bitcast(F32),
                 )
 
-        x_chunks = []
-        for c in range(X_CHUNKS):
-            x_chunk = chunks.tile([P, TOKEN_TILES, CHUNK_COLS], BF16, tag="chunk", name="x_chunk", align_bytes=64)
-            nc.sync.dma_start(
-                out=x_chunk[:], in_=x_view[:, :, CHUNK_COLS * c : CHUNK_COLS * (c + 1)]
-            )
-            x_chunks.append(x_chunk)
-            if c == 0:
-                nc.sync.dma_start(out=bias_rows[0:bo_rows, :], in_=bo.rearrange("(r c) -> r c", c=N_PASS))
-                nc.sync.dma_start(
-                    out=bias_rows[bo_rows : bo_rows + bg_rows, :], in_=bg.rearrange("(r c) -> r c", c=N_PASS)
-                )
+        x_tiles = [
+            chunks.tile([P, D], BF16, tag="chunk", name="x_tile", align_bytes=64)
+            for i in range(TOKEN_TILES)
+        ]
+
+        def load_x(i, part):
+            cols = slice(X_LOAD_COLS * part, X_LOAD_COLS * (part + 1))
+            nc.sync.dma_start(out=x_tiles[i][:, cols], in_=x_view[:, i, cols])
+
+        load_x(0, 0)
+        nc.sync.dma_start(out=bias_rows[0:bo_rows, :], in_=bo.rearrange("(r c) -> r c", c=N_PASS))
+        nc.sync.dma_start(
+            out=bias_rows[bo_rows : bo_rows + bg_rows, :], in_=bg.rearrange("(r c) -> r c", c=N_PASS)
+        )
+        load_x(1, 0)
+        load_x(0, 1)
+        load_x(1, 1)
 
         ret_sb = keep.tile([P, TOKEN_TILES, E], BF16)
         nc.sync.dma_start(out=ret_sb[:], in_=ret_view)
 
-        wg_chunks = []
-        for c in range(WG_CHUNKS):
-            wg_chunk = chunks.tile(
-                [P, WG_CHUNK_PASSES, E], U32, tag="chunk", name="wg_chunk", align_bytes=64
-            )
+        wg_tiles = []
+        for c in range(WG_LOADS):
+            first_pass = WG_LOAD_PASSES * c
+            slot = first_pass % WG_TILE_PASSES
+            if slot == 0:
+                wg_tile = chunks.tile(
+                    [P, WG_TILE_PASSES, E], U32, tag="chunk", name="wg_tile", align_bytes=64
+                )
+                wg_tiles.append(wg_tile)
             nc.sync.dma_start(
-                out=wg_chunk[:].bitcast(I32),
-                in_=wg_view[:, WG_CHUNK_PASSES * c : WG_CHUNK_PASSES * (c + 1), :].bitcast(I32),
+                out=wg_tiles[-1][:, slot : slot + WG_LOAD_PASSES, :].bitcast(I32),
+                in_=wg_view[:, first_pass : first_pass + WG_LOAD_PASSES, :].bitcast(I32),
             )
-            wg_chunks.append(wg_chunk)
 
         def spread_bias(first_row, dst):
             picked = work_pool.tile([P, 2 * N_PASS], BF16, tag="work", name="picked")
@@ -139,57 +147,54 @@ def tile_gatedmultiscaleretentionlayer_pa_k_kernel(
         def spread_bo(r):
             spread_bias(r, bo_all[:, N_PASS * r : N_PASS * (r + 2)])
 
-        def transpose_x_pass(g, grouped_words, copy):
-            c, g_in_chunk = divmod(g, PASSES_PER_X_CHUNK)
-            halves = work_pool.tile([P, 2, TOKENS], F32, tag="work", name="halves")
-            first_word = (K_PASS // 2) * g_in_chunk
-            for i in range(TOKEN_TILES):
-                words = x_chunks[c][:, i, :].bitcast(F32)
+        def transpose_x_passes(i, g, grouped_words, copy):
+            halves = work_pool.tile([P, 2, 2, P], F32, tag="work", name="halves")
+            words = x_tiles[i][:].bitcast(F32)
+            for j in range(2):
+                first_word = (K_PASS // 2) * (g + j)
                 for u in range(2):
                     nc.tensor.transpose(
-                        halves[:, u, P * i : P * (i + 1)],
+                        halves[:, j, u, :],
                         words[:, first_word + u : first_word + K_PASS // 2 : 2],
                         ident_f32[:],
                     )
             copy(
-                out=grouped_words.rearrange("p (w u) -> p w u", u=2),
-                in_=halves[:].rearrange("p u w -> p w u"),
+                out=grouped_words.rearrange("p (j w u) -> p j w u", j=2, u=2),
+                in_=halves[:].rearrange("p j u w -> p j w u"),
             )
 
-        def quantise_x_pair(pair, grouped):
-            passes = slice(2 * pair, 2 * pair + 2)
+        def quantise_x(i, g, grouped):
+            passes = slice(g, g + 4)
             nc.vector.quantize_mx(
-                out=x_codes[:, passes, :].rearrange("p g w -> p (g w)").bitcast(FP8X4),
-                scales=x_planes[:, passes, :].rearrange("p g w -> p (g w)"),
-                in_=grouped[:].rearrange("p g v -> p (g v)"),
+                out=x_codes[:, i, passes, :].rearrange("p g w -> p (g w)").bitcast(FP8X4),
+                scales=x_planes[:, i, passes, :].rearrange("p g w -> p (g w)"),
+                in_=grouped[:].rearrange("p j v -> p (j v)"),
             )
 
-        grouped_pairs = []
-        for pair in range(X_PASSES // 2):
-            grouped = stage.tile([P, 2, TOKENS * PACK], BF16, name="grouped", align_bytes=64)
-            grouped_pairs.append(grouped)
-            transpose_x_pass(2 * pair, grouped[:, 0, :].bitcast(F32), nc.scalar.copy)
-            transpose_x_pass(2 * pair + 1, grouped[:, 1, :].bitcast(F32), nc.vector.tensor_copy)
-            if pair > 0:
-                quantise_x_pair(pair - 1, grouped_pairs[pair - 1])
-            if pair == 1:
+        waiting = None
+        steps = [(i, g) for part in range(2) for i in range(TOKEN_TILES) for g in (8 * part, 8 * part + 4)]
+        for step, (i, g) in enumerate(steps):
+            grouped = stage.tile([P, 2, 2 * P * PACK], BF16, name="grouped", align_bytes=64)
+            transpose_x_passes(i, g, grouped[:, 0, :].bitcast(F32), nc.scalar.copy)
+            transpose_x_passes(i, g + 2, grouped[:, 1, :].bitcast(F32), nc.vector.tensor_copy)
+            if waiting is not None:
+                quantise_x(*waiting)
+            waiting = (i, g, grouped)
+            if step == 1:
                 spread_bias(bo_rows, bg_all[:])
-            if pair >= 2:
-                spread_bo(2 * (pair - 2))
-        quantise_x_pair(X_PASSES // 2 - 1, grouped_pairs[-1])
+            if step >= 2:
+                spread_bo(2 * (step - 2))
+        quantise_x(*waiting)
 
-        wo_chunks = []
-        for c in range(WO_CHUNKS):
-            wo_chunk = chunks.tile(
-                [P, H_PASSES, WO_CHUNK_COLS], U32, tag="chunk", name="wo_chunk", align_bytes=64
-            )
-            nc.sync.dma_start(
-                out=wo_chunk[:].bitcast(I32),
-                in_=wo_view[
-                    :, :, PACK * WO_CHUNK_COLS * c : PACK * WO_CHUNK_COLS * (c + 1)
-                ].bitcast(I32),
-            )
-            wo_chunks.append(wo_chunk)
+        wo_tiles = {}
+        for part in range(D // WO_COLS):
+            for g in range(H_PASSES):
+                wo_tile = chunks.tile([P, WO_COLS], U32, tag="chunk", name="wo_tile", align_bytes=64)
+                nc.sync.dma_start(
+                    out=wo_tile[:].bitcast(I32),
+                    in_=wo_view[:, g, PACK * WO_COLS * part : PACK * WO_COLS * (part + 1)].bitcast(I32),
+                )
+                wo_tiles[part, g] = wo_tile
 
         n_groups = TOKEN_TILES * E // GROUP
         by_group = ret_sb[:].rearrange("p i (h c) -> p (i h) c", c=GROUP)
@@ -234,24 +239,22 @@ def tile_gatedmultiscaleretentionlayer_pa_k_kernel(
         gate_acc = [
             acc_pool.tile([P, N_PASS], F32, tag="acc", name="gate_acc") for bank in gate_banks
         ]
-        for c in range(WG_CHUNKS):
-          wg_chunk = wg_chunks[c]
-          for acc, (i, b) in zip(gate_acc, gate_banks):
-            for g in range(WG_CHUNK_PASSES * c, WG_CHUNK_PASSES * (c + 1)):
-                block, plane = divmod(g, PLANES)
-                tokens = slice(P * i, P * (i + 1))
+        for c in range(WG_LOADS):
+            for acc, (i, b) in zip(gate_acc, gate_banks):
                 cols = slice(N_PASS * b, N_PASS * (b + 1))
-                nc.tensor.matmul_mx(
-                    out=acc[:],
-                    lhsT=x_codes[:, g, tokens].bitcast(FP8X4),
-                    lhsT_scale=x_planes[:, g, tokens],
-                    rhs=wg_chunk[:, g % WG_CHUNK_PASSES, cols].bitcast(FP8X4),
-                    rhs_scale=wg_planes[4 * plane : P, block, cols],
-                    start=(g == 0),
-                    stop=(g == X_PASSES - 1),
-                )
-          if c < 2:
-            spread_bo(12 + 2 * c)
+                for g in range(WG_LOAD_PASSES * c, WG_LOAD_PASSES * (c + 1)):
+                    block, plane = divmod(g, PLANES)
+                    nc.tensor.matmul_mx(
+                        out=acc[:],
+                        lhsT=x_codes[:, i, g, :].bitcast(FP8X4),
+                        lhsT_scale=x_planes[:, i, g, :],
+                        rhs=wg_tiles[g // WG_TILE_PASSES][:, g % WG_TILE_PASSES, cols].bitcast(FP8X4),
+                        rhs_scale=wg_planes[4 * plane : P, block, cols],
+                        start=(g == 0),
+                        stop=(g == X_PASSES - 1),
+                    )
+            if c < 2:
+                spread_bo(12 + 2 * c)
 
         gates = {}
         h_grouped = {}
@@ -290,42 +293,68 @@ def tile_gatedmultiscaleretentionlayer_pa_k_kernel(
                 in_=h_grouped[n][:].rearrange("p w t -> p (w t)"),
             )
 
-        n_banks = len(gate_banks)
-        for n in range(n_banks + 2):
-            if n < n_banks:
-                add_bias_and_silu(n)
-            if 1 <= n <= n_banks:
-                multiply_and_transpose(n - 1)
-            if n >= 2:
-                quantise_h(n - 2)
+        out_tiles = {}
 
-        for c in range(WO_CHUNKS):
-            out_chunk = chunks.tile(
-                [P, TOKEN_TILES, WO_CHUNK_COLS], F32, tag="chunk", name="out_chunk", align_bytes=64
+        def multiply_wo(i, bank):
+            first_col = N_PASS * bank
+            part, col = divmod(first_col, WO_COLS)
+            plane, plane_col = divmod(first_col, D // PLANES)
+            tokens = slice(P * i, P * (i + 1))
+            product = acc_pool.tile([P, N_PASS], F32, tag="acc", name="product")
+            for g in range(H_PASSES):
+                nc.tensor.matmul_mx(
+                    out=product[:],
+                    lhsT=h_codes[:, g, tokens].bitcast(FP8X4),
+                    lhsT_scale=h_planes[:, g, tokens],
+                    rhs=wo_tiles[part, g][:, col : col + N_PASS].bitcast(FP8X4),
+                    rhs_scale=wo_planes[4 * plane : P, g, plane_col : plane_col + N_PASS],
+                    start=(g == 0),
+                    stop=(g == H_PASSES - 1),
+                )
+            return product
+
+        def add_bo(i, bank, product):
+            first_col = N_PASS * bank
+            part, col = divmod(first_col, OUT_COLS)
+            if (i, part) not in out_tiles:
+                out_tile = chunks.tile([P, OUT_COLS], F32, tag="chunk", name="out_tile", align_bytes=64)
+                out_tiles[i, part] = out_tile
+            out_tile = out_tiles[i, part]
+            nc.vector.tensor_tensor(
+                out=out_tile[:, col : col + N_PASS],
+                in0=product[:],
+                in1=bo_all[:, first_col : first_col + N_PASS],
+                op=ADD,
             )
-            for i in range(TOKEN_TILES):
-                tokens = slice(P * i, P * (i + 1))
-                for b in range(WO_CHUNK_COLS // N_PASS):
-                    cols = slice(N_PASS * b, N_PASS * (b + 1))
-                    first_col = WO_CHUNK_COLS * c + N_PASS * b
-                    plane, plane_col = divmod(first_col, D // PLANES)
-                    product = acc_pool.tile([P, N_PASS], F32, tag="acc", name="product")
-                    for g in range(H_PASSES):
-                        nc.tensor.matmul_mx(
-                            out=product[:],
-                            lhsT=h_codes[:, g, tokens].bitcast(FP8X4),
-                            lhsT_scale=h_planes[:, g, tokens],
-                            rhs=wo_chunks[c][:, g, cols].bitcast(FP8X4),
-                            rhs_scale=wo_planes[4 * plane : P, g, plane_col : plane_col + N_PASS],
-                            start=(g == 0),
-                            stop=(g == H_PASSES - 1),
-                        )
-                    nc.vector.tensor_tensor(
-                        out=out_chunk[:, i, cols],
-                        in0=product[:],
-                        in1=bo_all[:, first_col : first_col + N_PASS],
-                        op=ADD,
-                    )
-            nc.sync.dma_start(
-                out=out_view[:, :, WO_CHUNK_COLS * c : WO_CHUNK_COLS * (c + 1)], in_=out_chunk[:]
-            )
+            end = first_col + N_PASS
+            if end % STORE_COLS == 0:
+                nc.sync.dma_start(
+                    out=out_view[:, i, end - STORE_COLS : end],
+                    in_=out_tile[:, col + N_PASS - STORE_COLS : col + N_PASS],
+                )
+
+        banks_per_part = WO_COLS // N_PASS
+        order = [
+            (i, bank)
+            for part in range(D // WO_COLS)
+            for i in range(TOKEN_TILES)
+            for bank in range(banks_per_part * part, banks_per_part * (part + 1))
+        ]
+        ahead = 2
+        add_bias_and_silu(0)
+        add_bias_and_silu(1)
+        multiply_and_transpose(0)
+        multiply_and_transpose(1)
+        quantise_h(0)
+        add_bias_and_silu(2)
+        quantise_h(1)
+        add_bias_and_silu(3)
+        products = [multiply_wo(*order[k]) for k in range(ahead)]
+        multiply_and_transpose(2)
+        multiply_and_transpose(3)
+        quantise_h(2)
+        quantise_h(3)
+        for k in range(len(order)):
+            if k + ahead < len(order):
+                products.append(multiply_wo(*order[k + ahead]))
+            add_bo(*order[k], products[k])

@@ -102,24 +102,25 @@ def tile_gatedmultiscaleretentionlayer_pa_k_kernel(
             for i in range(TOKEN_TILES)
         ]
 
-        def load_x(i, part):
-            cols = slice(X_LOAD_COLS * part, X_LOAD_COLS * (part + 1))
-            nc.sync.dma_start(out=x_tiles[i][:, cols], in_=x_view[:, i, cols])
+        def load_x(i, first, last):
+            nc.sync.dma_start(out=x_tiles[i][:, first:last], in_=x_view[:, i, first:last])
 
-        load_x(0, 0)
+        load_x(0, 0, X_LOAD_COLS // 2)
         nc.sync.dma_start(out=bias_rows[0:bo_rows, :], in_=bo.rearrange("(r c) -> r c", c=N_PASS))
         nc.sync.dma_start(
             out=bias_rows[bo_rows : bo_rows + bg_rows, :], in_=bg.rearrange("(r c) -> r c", c=N_PASS)
         )
-        load_x(1, 0)
-        load_x(0, 1)
-        load_x(1, 1)
+        load_x(0, X_LOAD_COLS // 2, X_LOAD_COLS)
+        load_x(1, 0, X_LOAD_COLS)
+        load_x(0, X_LOAD_COLS, D)
+        load_x(1, X_LOAD_COLS, D)
 
         ret_sb = keep.tile([P, TOKEN_TILES, E], BF16)
-        nc.sync.dma_start(out=ret_sb[:], in_=ret_view)
 
         wg_tiles = []
         for c in range(WG_LOADS):
+            if c == 2:
+                nc.sync.dma_start(out=ret_sb[:], in_=ret_view)
             first_pass = WG_LOAD_PASSES * c
             slot = first_pass % WG_TILE_PASSES
             if slot == 0:
@@ -176,15 +177,14 @@ def tile_gatedmultiscaleretentionlayer_pa_k_kernel(
         for step, (i, g) in enumerate(steps):
             grouped = stage.tile([P, 2, 2 * P * PACK], BF16, name="grouped", align_bytes=64)
             transpose_x_passes(i, g, grouped[:, 0, :].bitcast(F32), nc.scalar.copy)
-            transpose_x_passes(i, g + 2, grouped[:, 1, :].bitcast(F32), nc.vector.tensor_copy)
+            transpose_x_passes(
+                i, g + 2, grouped[:, 1, :].bitcast(F32), nc.scalar.copy if step % 2 else nc.vector.tensor_copy
+            )
             if waiting is not None:
                 quantise_x(*waiting)
             waiting = (i, g, grouped)
-            if step == 1:
-                spread_bias(bo_rows, bg_all[:])
-            if step >= 2:
-                spread_bo(2 * (step - 2))
         quantise_x(*waiting)
+        spread_bias(bo_rows, bg_all[:])
 
         wo_tiles = {}
         for part in range(D // WO_COLS):
@@ -253,8 +253,8 @@ def tile_gatedmultiscaleretentionlayer_pa_k_kernel(
                         start=(g == 0),
                         stop=(g == X_PASSES - 1),
                     )
-            if c < 2:
-                spread_bo(12 + 2 * c)
+            if c < WG_LOADS - 1:
+                spread_bo(2 * c)
 
         gates = {}
         h_grouped = {}
@@ -352,6 +352,7 @@ def tile_gatedmultiscaleretentionlayer_pa_k_kernel(
         products = [multiply_wo(*order[k]) for k in range(ahead)]
         multiply_and_transpose(2)
         multiply_and_transpose(3)
+        spread_bo(bo_rows - 2)
         quantise_h(2)
         quantise_h(3)
         for k in range(len(order)):

@@ -82,20 +82,28 @@ def tile_gatedmultiscaleretentionlayer_pa_k_kernel(
 
         bo_rows = D // N_PASS
         bg_rows = E // N_PASS
-        for a in range(X_PASSES // PLANES):
-            for q in range(QUADS):
-                nc.gpsimd.dma_start(
-                    out=wg_planes[32 * q : 32 * q + 16, a, :].bitcast(F32),
-                    in_=Wg_scales[PLANES * a : PLANES * (a + 1), 4 * q : 4 * q + 4, :].bitcast(F32),
+        def load_wg_scales(queue, a, quads, dtype):
+            for q in quads:
+                queue.dma_start(
+                    out=wg_planes[32 * q : 32 * q + 16, a, :].bitcast(dtype),
+                    in_=Wg_scales[PLANES * a : PLANES * (a + 1), 4 * q : 4 * q + 4, :].bitcast(dtype),
                 )
-        for g in range(H_PASSES):
-            for q in range(QUADS):
-                nc.gpsimd.dma_start(
-                    out=wo_planes[32 * q : 32 * q + 16, g, :].bitcast(F32),
+
+        def load_wo_scales(queue, g, quads, dtype):
+            for q in quads:
+                queue.dma_start(
+                    out=wo_planes[32 * q : 32 * q + 16, g, :].bitcast(dtype),
                     in_=Wo_scales[g, 4 * q : 4 * q + 4, :]
                     .rearrange("r (j n) -> j r n", j=PLANES)
-                    .bitcast(F32),
+                    .bitcast(dtype),
                 )
+
+        sync_quads = (0, 1)
+        gpsimd_quads = (2, 3)
+        for a in range(X_PASSES // PLANES):
+            load_wg_scales(nc.gpsimd, a, gpsimd_quads, F32)
+        for g in range(H_PASSES):
+            load_wo_scales(nc.gpsimd, g, gpsimd_quads, F32)
 
         x_tiles = [
             chunks.tile([P, D], BF16, tag="chunk", name="x_tile", align_bytes=64)
@@ -112,8 +120,10 @@ def tile_gatedmultiscaleretentionlayer_pa_k_kernel(
         )
         load_x(0, X_LOAD_COLS // 2, X_LOAD_COLS)
         load_x(1, 0, X_LOAD_COLS)
+        load_wg_scales(nc.sync, 0, sync_quads, I32)
         load_x(0, X_LOAD_COLS, D)
         load_x(1, X_LOAD_COLS, D)
+        load_wg_scales(nc.sync, 1, sync_quads, I32)
 
         ret_sb = keep.tile([P, TOKEN_TILES, E], BF16)
 
@@ -121,6 +131,9 @@ def tile_gatedmultiscaleretentionlayer_pa_k_kernel(
         for c in range(WG_LOADS):
             if c == 2:
                 nc.sync.dma_start(out=ret_sb[:], in_=ret_view)
+                load_wg_scales(nc.sync, 2, sync_quads, I32)
+            if c == 4:
+                load_wg_scales(nc.sync, 3, sync_quads, I32)
             first_pass = WG_LOAD_PASSES * c
             slot = first_pass % WG_TILE_PASSES
             if slot == 0:
@@ -187,6 +200,8 @@ def tile_gatedmultiscaleretentionlayer_pa_k_kernel(
         spread_bias(bo_rows, bg_all[:])
 
         wo_tiles = {}
+        for g in range(H_PASSES):
+            load_wo_scales(nc.sync, g, sync_quads, I32)
         for part in range(D // WO_COLS):
             for g in range(H_PASSES):
                 wo_tile = chunks.tile([P, WO_COLS], U32, tag="chunk", name="wo_tile", align_bytes=64)
@@ -214,26 +229,28 @@ def tile_gatedmultiscaleretentionlayer_pa_k_kernel(
         squares = keep.tile([P, n_groups, GROUP], F32)
         nc.scalar.activation(out=squares[:], in_=cat[:], func=ACT.Square)
         square_sums = keep.tile([P, n_groups], F32)
-        nc.vector.tensor_reduce(
-            out=square_sums[:], in_=squares[:], axis=mybir.AxisListType.X, op=ADD
-        )
         var_eps = keep.tile([P, n_groups], F32)
-        nc.vector.tensor_scalar(
-            out=var_eps[:], in0=square_sums[:], scalar1=1.0 / GROUP, scalar2=EPS, op0=MULT, op1=ADD
-        )
         std = keep.tile([P, n_groups], F32)
-        nc.scalar.activation(out=std[:], in_=var_eps[:], func=ACT.Sqrt)
         table_warmer = keep.tile([P, 1], F32)
-        nc.scalar.activation(out=table_warmer[:], in_=std[:, 0:1], func=ACT.Silu)
         inv_std = keep.tile([P, n_groups], F32)
-        nc.vector.reciprocal(out=inv_std[:], in_=std[:])
-        nc.vector.tensor_tensor(
-            out=cat[:],
-            in0=cat[:],
-            in1=inv_std[:].unsqueeze(2).to_broadcast([P, n_groups, GROUP]),
-            op=MULT,
-        )
         cat_flat = cat[:].rearrange("p (i h) c -> p i (h c)", i=TOKEN_TILES)
+
+        def finish_norm():
+            nc.vector.tensor_reduce(
+                out=square_sums[:], in_=squares[:], axis=mybir.AxisListType.X, op=ADD
+            )
+            nc.vector.tensor_scalar(
+                out=var_eps[:], in0=square_sums[:], scalar1=1.0 / GROUP, scalar2=EPS, op0=MULT, op1=ADD
+            )
+            nc.scalar.activation(out=std[:], in_=var_eps[:], func=ACT.Sqrt)
+            nc.scalar.activation(out=table_warmer[:], in_=std[:, 0:1], func=ACT.Silu)
+            nc.vector.reciprocal(out=inv_std[:], in_=std[:])
+            nc.vector.tensor_tensor(
+                out=cat[:],
+                in0=cat[:],
+                in1=inv_std[:].unsqueeze(2).to_broadcast([P, n_groups, GROUP]),
+                op=MULT,
+            )
 
         gate_banks = [(i, b) for i in range(TOKEN_TILES) for b in range(E_BANKS)]
         gate_acc = [
@@ -253,8 +270,10 @@ def tile_gatedmultiscaleretentionlayer_pa_k_kernel(
                         start=(g == 0),
                         stop=(g == X_PASSES - 1),
                     )
-            if c < WG_LOADS - 1:
+            if c < 4:
                 spread_bo(2 * c)
+            if c == 4:
+                finish_norm()
 
         gates = {}
         h_grouped = {}
@@ -340,22 +359,33 @@ def tile_gatedmultiscaleretentionlayer_pa_k_kernel(
             for i in range(TOKEN_TILES)
             for bank in range(banks_per_part * part, banks_per_part * (part + 1))
         ]
-        ahead = 2
+        products = []
+
+        def multiply_next():
+            products.append(multiply_wo(*order[len(products)]))
+
         add_bias_and_silu(0)
         add_bias_and_silu(1)
+        add_bias_and_silu(2)
+        spread_bo(8)
         multiply_and_transpose(0)
         multiply_and_transpose(1)
-        quantise_h(0)
-        add_bias_and_silu(2)
-        quantise_h(1)
         add_bias_and_silu(3)
-        products = [multiply_wo(*order[k]) for k in range(ahead)]
+        quantise_h(0)
+        spread_bo(10)
         multiply_and_transpose(2)
+        quantise_h(1)
+        multiply_next()
         multiply_and_transpose(3)
-        spread_bo(bo_rows - 2)
         quantise_h(2)
-        quantise_h(3)
+        multiply_next()
         for k in range(len(order)):
-            if k + ahead < len(order):
-                products.append(multiply_wo(*order[k + ahead]))
+            if len(products) < len(order):
+                multiply_next()
             add_bo(*order[k], products[k])
+            if k == 0:
+                quantise_h(3)
+            if k == 4:
+                spread_bo(12)
+            if k == 8:
+                spread_bo(14)

from contextlib import ExitStack

import concourse.mybir as mybir
from concourse.masks import make_identity

F32 = mybir.dt.float32
BF16 = mybir.dt.bfloat16
I32 = mybir.dt.int32
U32 = mybir.dt.uint32
U8 = mybir.dt.uint8
FP8X4 = mybir.dt.float8_e4m3fn_x4
ADD = mybir.AluOpType.add
MULT = mybir.AluOpType.mult
ACT = mybir.ActivationFunctionType

P = 128
PACK = 4
K_PASS = P * PACK
N_PASS = 512

TOKENS = 256
TOKEN_TILES = TOKENS // P
D = 8192
E = 1024
GROUP = 128
EPS = 1e-5

X_PASSES = D // K_PASS
H_PASSES = E // K_PASS
E_BANKS = E // N_PASS
PLANES = 4
QUADS = 4

X_LOAD_COLS = 4096
WG_TILE_PASSES = 4
WG_LOAD_PASSES = 2
WG_LOADS = X_PASSES // WG_LOAD_PASSES
WO_COLS = 4096
OUT_COLS = 4096
STORE_COLS = 2048

FLOPS = 2 * TOKENS * D * E * 2


def tile_gatedmultiscaleretentionlayer_pa_k_kernel(
    tc, x, ret_cat, Wg_words, Wg_scales, bg, Wo_words, Wo_scales, bo, out
):
    nc = tc.nc

    x_view = x.rearrange("b s d -> (b s) d").rearrange("(i p) d -> p i d", p=P)
    ret_view = ret_cat.rearrange("b s e -> (b s) e").rearrange("(i p) e -> p i e", p=P)
    out_view = out.rearrange("b s d -> (b s) d").rearrange("(i p) d -> p i d", p=P)
    wg_view = Wg_words.rearrange("g p n t -> p g (n t)")
    wo_view = Wo_words.rearrange("g p n t -> p g (n t)")

    with ExitStack() as stack:
        stack.enter_context(tc.manual_schedule())
        keep = stack.enter_context(tc.tile_pool(name="keep", bufs=1))
        chunks = stack.enter_context(tc.tile_pool(name="chunks", bufs=8))
        stage = stack.enter_context(tc.tile_pool(name="stage", bufs=3))
        acc_pool = stack.enter_context(tc.psum_pool(name="acc", bufs=4))
        work_pool = stack.enter_context(tc.psum_pool(name="work", bufs=4))

        bias_rows = keep.tile([P, N_PASS], BF16)
        nc.vector.memset(bias_rows[:], 0.0)
        wg_planes = keep.tile([P, X_PASSES // PLANES, E], U8, align_bytes=64)
        wo_planes = keep.tile([P, H_PASSES, D // PLANES], U8, align_bytes=64)
        nc.vector.memset(wg_planes[:].rearrange("p a n -> p (a n)").bitcast(I32), 0)
        nc.vector.memset(wo_planes[:].rearrange("p a n -> p (a n)").bitcast(I32), 0)

        ident_bf = keep.tile([P, P], BF16)
        make_identity(nc, ident_bf[:])
        ident_f32 = keep.tile([P, P], F32)
        make_identity(nc, ident_f32[:])

        x_codes = keep.tile([P, TOKEN_TILES, X_PASSES, P], U32, align_bytes=64)
        x_planes = keep.tile([P, TOKEN_TILES, X_PASSES, P], U8, align_bytes=64)
        h_codes = keep.tile([P, H_PASSES, TOKENS], U32, align_bytes=64)
        h_planes = keep.tile([P, H_PASSES, TOKENS], U8, align_bytes=64)
        bo_all = keep.tile([P, D], BF16)
        bg_all = keep.tile([P, E], BF16)

        bo_rows = D // N_PASS
        bg_rows = E // N_PASS
        def load_wg_scales(queue, a, quads, dtype):
            for q in quads:
                queue.dma_start(
                    out=wg_planes[32 * q : 32 * q + 16, a, :].bitcast(dtype),
                    in_=Wg_scales[PLANES * a : PLANES * (a + 1), 4 * q : 4 * q + 4, :].bitcast(dtype),
                )

        def load_wo_scales(queue, g, quads, dtype):
            for q in quads:
                queue.dma_start(
                    out=wo_planes[32 * q : 32 * q + 16, g, :].bitcast(dtype),
                    in_=Wo_scales[g, 4 * q : 4 * q + 4, :]
                    .rearrange("r (j n) -> j r n", j=PLANES)
                    .bitcast(dtype),
                )

        sync_quads = (0, 1)
        gpsimd_quads = (2, 3)
        for a in range(X_PASSES // PLANES):
            load_wg_scales(nc.gpsimd, a, gpsimd_quads, F32)
        for g in range(H_PASSES):
            load_wo_scales(nc.gpsimd, g, gpsimd_quads, F32)

        x_tiles = [
            chunks.tile([P, D], BF16, tag="chunk", name="x_tile", align_bytes=64)
            for i in range(TOKEN_TILES)
        ]

        def load_x(i, first, last):
            nc.sync.dma_start(out=x_tiles[i][:, first:last], in_=x_view[:, i, first:last])

        load_x(0, 0, X_LOAD_COLS // 2)
        nc.sync.dma_start(out=bias_rows[0:bo_rows, :], in_=bo.rearrange("(r c) -> r c", c=N_PASS))
        nc.sync.dma_start(
            out=bias_rows[bo_rows : bo_rows + bg_rows, :], in_=bg.rearrange("(r c) -> r c", c=N_PASS)
        )
        load_x(0, X_LOAD_COLS // 2, X_LOAD_COLS)
        load_x(1, 0, X_LOAD_COLS)
        load_wg_scales(nc.sync, 0, sync_quads, I32)
        load_x(0, X_LOAD_COLS, D)
        load_x(1, X_LOAD_COLS, D)
        load_wg_scales(nc.sync, 1, sync_quads, I32)

        ret_sb = keep.tile([P, TOKEN_TILES, E], BF16)

        wg_tiles = []
        for c in range(WG_LOADS):
            if c == 2:
                nc.sync.dma_start(out=ret_sb[:], in_=ret_view)
                load_wg_scales(nc.sync, 2, sync_quads, I32)
            if c == 4:
                load_wg_scales(nc.sync, 3, sync_quads, I32)
            first_pass = WG_LOAD_PASSES * c
            slot = first_pass % WG_TILE_PASSES
            if slot == 0:
                wg_tile = chunks.tile(
                    [P, WG_TILE_PASSES, E], U32, tag="chunk", name="wg_tile", align_bytes=64
                )
                wg_tiles.append(wg_tile)
            nc.sync.dma_start(
                out=wg_tiles[-1][:, slot : slot + WG_LOAD_PASSES, :].bitcast(I32),
                in_=wg_view[:, first_pass : first_pass + WG_LOAD_PASSES, :].bitcast(I32),
            )

        def spread_bias(first_row, dst):
            picked = work_pool.tile([P, 2 * N_PASS], BF16, tag="work", name="picked")
            for i in range(2):
                nc.tensor.matmul(
                    out=picked[:, N_PASS * i : N_PASS * (i + 1)],
                    lhsT=ident_bf[:, first_row + i : first_row + i + 1].to_broadcast([P, P]),
                    rhs=bias_rows[:],
                    start=True,
                    stop=True,
                )
            nc.scalar.copy(out=dst, in_=picked[:])

        def spread_bo(r):
            spread_bias(r, bo_all[:, N_PASS * r : N_PASS * (r + 2)])

        def transpose_x_passes(i, g, grouped_words, copy):
            halves = work_pool.tile([P, 2, 2, P], F32, tag="work", name="halves")
            words = x_tiles[i][:].bitcast(F32)
            for j in range(2):
                first_word = (K_PASS // 2) * (g + j)
                for u in range(2):
                    nc.tensor.transpose(
                        halves[:, j, u, :],
                        words[:, first_word + u : first_word + K_PASS // 2 : 2],
                        ident_f32[:],
                    )
            copy(
                out=grouped_words.rearrange("p (j w u) -> p j w u", j=2, u=2),
                in_=halves[:].rearrange("p j u w -> p j w u"),
            )

        def quantise_x(i, g, grouped):
            passes = slice(g, g + 4)
            nc.vector.quantize_mx(
                out=x_codes[:, i, passes, :].rearrange("p g w -> p (g w)").bitcast(FP8X4),
                scales=x_planes[:, i, passes, :].rearrange("p g w -> p (g w)"),
                in_=grouped[:].rearrange("p j v -> p (j v)"),
            )

        waiting = None
        steps = [(i, g) for part in range(2) for i in range(TOKEN_TILES) for g in (8 * part, 8 * part + 4)]
        for step, (i, g) in enumerate(steps):
            grouped = stage.tile([P, 2, 2 * P * PACK], BF16, name="grouped", align_bytes=64)
            transpose_x_passes(i, g, grouped[:, 0, :].bitcast(F32), nc.scalar.copy)
            transpose_x_passes(
                i, g + 2, grouped[:, 1, :].bitcast(F32), nc.scalar.copy if step % 2 else nc.vector.tensor_copy
            )
            if waiting is not None:
                quantise_x(*waiting)
            waiting = (i, g, grouped)
        quantise_x(*waiting)
        spread_bias(bo_rows, bg_all[:])

        wo_tiles = {}
        for g in range(H_PASSES):
            load_wo_scales(nc.sync, g, sync_quads, I32)
        for part in range(D // WO_COLS):
            for g in range(H_PASSES):
                wo_tile = chunks.tile([P, WO_COLS], U32, tag="chunk", name="wo_tile", align_bytes=64)
                nc.sync.dma_start(
                    out=wo_tile[:].bitcast(I32),
                    in_=wo_view[:, g, PACK * WO_COLS * part : PACK * WO_COLS * (part + 1)].bitcast(I32),
                )
                wo_tiles[part, g] = wo_tile

        n_groups = TOKEN_TILES * E // GROUP
        by_group = ret_sb[:].rearrange("p i (h c) -> p (i h) c", c=GROUP)
        sums = keep.tile([P, n_groups], F32)
        nc.vector.tensor_reduce(out=sums[:], in_=by_group, axis=mybir.AxisListType.X, op=ADD)
        neg_mean = keep.tile([P, n_groups], F32)
        nc.vector.tensor_scalar(
            out=neg_mean[:], in0=sums[:], scalar1=-1.0 / GROUP, scalar2=None, op0=MULT
        )
        cat = keep.tile([P, n_groups, GROUP], F32)
        nc.vector.tensor_tensor(
            out=cat[:],
            in0=by_group,
            in1=neg_mean[:].unsqueeze(2).to_broadcast([P, n_groups, GROUP]),
            op=ADD,
        )
        squares = keep.tile([P, n_groups, GROUP], F32)
        nc.scalar.activation(out=squares[:], in_=cat[:], func=ACT.Square)
        square_sums = keep.tile([P, n_groups], F32)
        var_eps = keep.tile([P, n_groups], F32)
        std = keep.tile([P, n_groups], F32)
        table_warmer = keep.tile([P, 1], F32)
        inv_std = keep.tile([P, n_groups], F32)
        cat_flat = cat[:].rearrange("p (i h) c -> p i (h c)", i=TOKEN_TILES)

        def finish_norm():
            nc.vector.tensor_reduce(
                out=square_sums[:], in_=squares[:], axis=mybir.AxisListType.X, op=ADD
            )
            nc.vector.tensor_scalar(
                out=var_eps[:], in0=square_sums[:], scalar1=1.0 / GROUP, scalar2=EPS, op0=MULT, op1=ADD
            )
            nc.scalar.activation(out=std[:], in_=var_eps[:], func=ACT.Sqrt)
            nc.scalar.activation(out=table_warmer[:], in_=std[:, 0:1], func=ACT.Silu)
            nc.vector.reciprocal(out=inv_std[:], in_=std[:])
            nc.vector.tensor_tensor(
                out=cat[:],
                in0=cat[:],
                in1=inv_std[:].unsqueeze(2).to_broadcast([P, n_groups, GROUP]),
                op=MULT,
            )

        gate_banks = [(i, b) for i in range(TOKEN_TILES) for b in range(E_BANKS)]
        gate_acc = [
            acc_pool.tile([P, N_PASS], F32, tag="acc", name="gate_acc") for bank in gate_banks
        ]
        for c in range(WG_LOADS):
            for acc, (i, b) in zip(gate_acc, gate_banks):
                cols = slice(N_PASS * b, N_PASS * (b + 1))
                for g in range(WG_LOAD_PASSES * c, WG_LOAD_PASSES * (c + 1)):
                    block, plane = divmod(g, PLANES)
                    nc.tensor.matmul_mx(
                        out=acc[:],
                        lhsT=x_codes[:, i, g, :].bitcast(FP8X4),
                        lhsT_scale=x_planes[:, i, g, :],
                        rhs=wg_tiles[g // WG_TILE_PASSES][:, g % WG_TILE_PASSES, cols].bitcast(FP8X4),
                        rhs_scale=wg_planes[4 * plane : P, block, cols],
                        start=(g == 0),
                        stop=(g == X_PASSES - 1),
                    )
            if c < 4:
                spread_bo(2 * c)
            if c == 4:
                finish_norm()

        gates = {}
        h_grouped = {}

        def add_bias_and_silu(n):
            i, b = gate_banks[n]
            gate = stage.tile([P, N_PASS], F32, name="gate")
            nc.vector.tensor_tensor(
                out=gate[:], in0=gate_acc[n][:], in1=bg_all[:, N_PASS * b : N_PASS * (b + 1)], op=ADD
            )
            nc.scalar.activation(out=gate[:], in_=gate[:], func=ACT.Silu)
            gates[n] = gate

        def multiply_and_transpose(n):
            i, b = gate_banks[n]
            h_runs = stage.tile([P, PACK, P], BF16, name="h_runs")
            nc.vector.tensor_tensor(
                out=h_runs[:],
                in0=gates[n][:].rearrange("p (c t) -> p t c", t=PACK),
                in1=cat_flat[:, i, N_PASS * b : N_PASS * (b + 1)].rearrange("p (c t) -> p t c", t=PACK),
                op=MULT,
            )
            flipped = work_pool.tile([P, PACK, P], BF16, tag="work", name="flipped")
            for t in range(PACK):
                nc.tensor.transpose(flipped[:, t, :], h_runs[:, t, :], ident_bf[:])
            grouped_h = stage.tile([P, P, PACK], BF16, name="grouped_h", align_bytes=64)
            nc.scalar.copy(out=grouped_h[:], in_=flipped[:].rearrange("p t w -> p w t"))
            h_grouped[n] = grouped_h

        def quantise_h(n):
            i, b = gate_banks[n]
            tokens = slice(P * i, P * (i + 1))
            nc.vector.quantize_mx(
                out=h_codes[:, b, tokens].bitcast(FP8X4),
                scales=h_planes[:, b, tokens],
                in_=h_grouped[n][:].rearrange("p w t -> p (w t)"),
            )

        out_tiles = {}

        def multiply_wo(i, bank):
            first_col = N_PASS * bank
            part, col = divmod(first_col, WO_COLS)
            plane, plane_col = divmod(first_col, D // PLANES)
            tokens = slice(P * i, P * (i + 1))
            product = acc_pool.tile([P, N_PASS], F32, tag="acc", name="product")
            for g in range(H_PASSES):
                nc.tensor.matmul_mx(
                    out=product[:],
                    lhsT=h_codes[:, g, tokens].bitcast(FP8X4),
                    lhsT_scale=h_planes[:, g, tokens],
                    rhs=wo_tiles[part, g][:, col : col + N_PASS].bitcast(FP8X4),
                    rhs_scale=wo_planes[4 * plane : P, g, plane_col : plane_col + N_PASS],
                    start=(g == 0),
                    stop=(g == H_PASSES - 1),
                )
            return product

        def add_bo(i, bank, product):
            first_col = N_PASS * bank
            part, col = divmod(first_col, OUT_COLS)
            if (i, part) not in out_tiles:
                out_tile = chunks.tile([P, OUT_COLS], F32, tag="chunk", name="out_tile", align_bytes=64)
                out_tiles[i, part] = out_tile
            out_tile = out_tiles[i, part]
            nc.vector.tensor_tensor(
                out=out_tile[:, col : col + N_PASS],
                in0=product[:],
                in1=bo_all[:, first_col : first_col + N_PASS],
                op=ADD,
            )
            end = first_col + N_PASS
            if end % STORE_COLS == 0:
                nc.sync.dma_start(
                    out=out_view[:, i, end - STORE_COLS : end],
                    in_=out_tile[:, col + N_PASS - STORE_COLS : col + N_PASS],
                )

        banks_per_part = WO_COLS // N_PASS
        order = [
            (i, bank)
            for part in range(D // WO_COLS)
            for i in range(TOKEN_TILES)
            for bank in range(banks_per_part * part, banks_per_part * (part + 1))
        ]
        products = []

        def multiply_next():
            products.append(multiply_wo(*order[len(products)]))

        add_bias_and_silu(0)
        add_bias_and_silu(1)
        add_bias_and_silu(2)
        spread_bo(8)
        multiply_and_transpose(0)
        multiply_and_transpose(1)
        add_bias_and_silu(3)
        quantise_h(0)
        spread_bo(10)
        multiply_and_transpose(2)
        quantise_h(1)
        multiply_next()
        multiply_and_transpose(3)
        quantise_h(2)
        multiply_next()
        for k in range(len(order)):
            if len(products) < len(order):
                multiply_next()
            add_bo(*order[k], products[k])
            if k == 0:
                quantise_h(3)
            if k == 4:
                spread_bo(12)
            if k == 8:
                spread_bo(14)
